import numpy as np
import ml_dtypes

BF16 = ml_dtypes.bfloat16


def bf(x):
    return np.asarray(x, np.float32).astype(BF16)


def f32(x):
    return np.asarray(x, np.float32)


def f64(x):
    return np.asarray(x).astype(np.float64)


def striped(idx):
    return np.tile(idx.reshape(-1, 16).T, (8, 1))


V, E, N, W = 512, 128, 1024, 128


def setup_inputs():
    return {"table": bf(np.random.standard_normal((V, E))), "wq": bf(1.2 * np.random.standard_normal((E, E)) / np.sqrt(E)), "wk": bf(1.2 * np.random.standard_normal((E, E)) / np.sqrt(E)), "wv": bf(2.0 * np.random.standard_normal((E, E)) / np.sqrt(E)), "bq": f32(0.1 * np.random.standard_normal((E, 1))), "bv": f32(0.1 * np.random.standard_normal((E, 1))), "offs": striped(np.random.permutation(np.tile(np.arange(V), 2))[:N])}


def reference(table, wq, wk, wv, bq, bv, offs):
    idx = offs[:16].T.reshape(-1)
    h = f64(table)[idx].T
    q = (f64(wq).T @ h + f64(bq)) / np.sqrt(E)
    key = f64(wk).T @ h
    v = f64(wv).T @ h + f64(bv)
    score = q.T @ key
    pos = np.arange(N)
    band = np.abs(pos[:, None] - pos[None, :]) <= W
    score = np.where(band, score, -1e30)
    e = np.exp(score - score.max(axis=1, keepdims=True))
    p = e / e.sum(axis=1, keepdims=True)
    return v @ p.T

@@ -1,0 +1,151 @@
+import math
+
+import concourse.mybir as mybir
+from concourse.masks import make_identity
+
+BF16, F32, I32, U16 = mybir.dt.bfloat16, mybir.dt.float32, mybir.dt.int32, mybir.dt.uint16
+ADD, MULT, IS_GT = mybir.AluOpType.add, mybir.AluOpType.mult, mybir.AluOpType.is_gt
+EXP = mybir.ActivationFunctionType.Exp
+IDENTITY = mybir.ActivationFunctionType.Identity
+ALONG_FREE = mybir.AxisListType.X
+
+P = 128
+V, E, N = 512, 128, 1024
+W = 128
+PIECE = 512
+N_PIECES = N // PIECE
+N_BLOCKS = N // P
+BLOCKS_PER_PIECE = PIECE // P
+MASKED = -1.0e30
+
+PAIRS_IN_BAND = N * (2 * W + 1) - W * (W + 1)
+FLOPS = 3 * 2 * E * E * N + 2 * 2 * E * PAIRS_IN_BAND
+
+
+def tile_longformerselfattention_kernel(tc, table, wq, wk, wv, bq, bv, offs, out):
+    nc = tc.nc
+    with (
+        tc.tile_pool(name="lists", bufs=1) as lists,
+        tc.tile_pool(name="held", bufs=1) as held,
+        tc.tile_pool(name="work", bufs=3) as work,
+        tc.tile_pool(name="stats", bufs=4) as stats,
+        tc.psum_pool(name="products", bufs=4) as products,
+        tc.psum_pool(name="flipped", bufs=2) as flipped,
+        tc.psum_pool(name="sums", bufs=2) as sums,
+    ):
+        table_rows = held.tile([P, V // P, E], BF16, name="table_rows")
+        table_view = table.rearrange("(r p) d -> p r d", p=P)
+        nc.sync.dma_start(table_rows[:, 0:2, :], table_view[:, 0:2, :])
+        nc.scalar.dma_start(table_rows[:, 2:4, :], table_view[:, 2:4, :])
+        offsets = lists.tile([P, N // 16], U16, name="offsets")
+        nc.sync.dma_start(offsets[:], offs)
+        wq_sb = held.tile([E, E], BF16, name="wq_sb")
+        wk_sb = held.tile([E, E], BF16, name="wk_sb")
+        wv_sb = held.tile([E, E], BF16, name="wv_sb")
+        nc.scalar.dma_start(wq_sb[:], wq)
+        nc.sync.dma_start(wk_sb[:], wk)
+        nc.scalar.dma_start(wv_sb[:], wv)
+        bq_sb = held.tile([E, 1], F32, name="bq_sb")
+        bv_sb = held.tile([E, 1], F32, name="bv_sb")
+        with nc.allow_non_contiguous_dma(reason="one float32 of a bias to each partition"):
+            nc.sync.dma_start(bq_sb[:], bq)
+            nc.scalar.dma_start(bv_sb[:], bv)
+
+        warm = stats.tile([P, 1], F32, name="warm")
+        nc.vector.memset(warm[:], 0.0)
+        nc.scalar.activation(warm[:], warm[:], EXP)
+
+        ident = held.tile([P, P], BF16, name="ident")
+        make_identity(nc, ident[:])
+        distance = held.tile([P, 3 * P], I32, name="distance")
+        nc.gpsimd.iota(distance[:], pattern=[[1, 3 * P]], base=-P, channel_multiplier=-1)
+        distance_sq = held.tile([P, 3 * P], F32, name="distance_sq")
+        nc.vector.tensor_tensor(distance_sq[:], distance[:], distance[:], MULT)
+        band_mask = held.tile([P, 3 * P], BF16, name="band_mask")
+        nc.vector.tensor_scalar(band_mask[:], distance_sq[:], float(W * W), MASKED, op0=IS_GT, op1=MULT)
+
+        tableT_ps = flipped.tile([E, V], BF16, name="tableT_ps", tag="flipped")
+        for r in range(V // P):
+            nc.tensor.transpose(tableT_ps[:, r * P : (r + 1) * P], table_rows[:, r, :], ident[:])
+        tableT = held.tile([E, V], BF16, name="tableT")
+        nc.vector.tensor_copy(tableT[:], tableT_ps[:])
+
+        q_sb = held.tile([E, N], BF16, name="q_sb")
+        key_sb = held.tile([E, N], BF16, name="key_sb")
+        v_sb = held.tile([E, N], BF16, name="v_sb")
+        def project(weights, piece):
+            looked_up = tableT[:].indirect(offsets[:, piece * (PIECE // 16) : (piece + 1) * (PIECE // 16)])
+            product = products.tile([E, PIECE], F32, name="product", tag="product")
+            nc.tensor.matmul(product[:], weights[:], looked_up, start=True, stop=True)
+            return product
+
+        pieces = [slice(piece * PIECE, (piece + 1) * PIECE) for piece in range(N_PIECES)]
+        for piece, cols in enumerate(pieces):
+            nc.vector.tensor_scalar(
+                q_sb[:, cols], project(wq_sb, piece)[:], bq_sb[:], 1.0 / math.sqrt(E), op0=ADD, op1=MULT
+            )
+        for piece, cols in enumerate(pieces):
+            nc.scalar.copy(key_sb[:, cols], project(wk_sb, piece)[:])
+        for piece, cols in enumerate(pieces):
+            nc.scalar.activation(v_sb[:, cols], project(wv_sb, piece)[:], IDENTITY, bias=bv_sb[:], scale=1.0)
+
+        vT = held.tile([P, N], BF16, name="vT")
+        for piece in range(N_PIECES):
+            vT_ps = flipped.tile([P, PIECE], BF16, name="vT_ps", tag="flipped")
+            for b in range(BLOCKS_PER_PIECE):
+                block = piece * BLOCKS_PER_PIECE + b
+                nc.tensor.transpose(vT_ps[:, b * P : (b + 1) * P], v_sb[:, block * P : (block + 1) * P], ident[:])
+            nc.vector.tensor_copy(vT[:, piece * PIECE : (piece + 1) * PIECE], vT_ps[:])
+
+        out_sb = held.tile([E, N], F32, name="out_sb")
+        for piece in range(N_PIECES):
+            out_ps = sums.tile([E, PIECE], F32, name="out_ps", tag="out_ps")
+            for b in range(BLOCKS_PER_PIECE):
+                block = piece * BLOCKS_PER_PIECE + b
+                first, last = max(block - 1, 0), min(block + 1, N_BLOCKS - 1)
+                key_blocks = list(range(first, last + 1))
+                width = len(key_blocks) * P
+                mask_from = (first - (block - 1)) * P
+
+                scores = products.tile([P, 3 * P], F32, name="scores", tag="product")
+                nc.tensor.matmul(
+                    scores[:, :width],
+                    q_sb[:, block * P : (block + 1) * P],
+                    key_sb[:, first * P : (last + 1) * P],
+                    start=True,
+                    stop=False,
+                )
+                nc.tensor.matmul(
+                    scores[:, :width], ident[:], band_mask[:, mask_from : mask_from + width], start=False, stop=True
+                )
+
+                neg_max = stats.tile([P, 1], F32, name="neg_max")
+                nc.vector.reduce_max(neg_max[:], scores[:, :width], axis=ALONG_FREE, negate=True)
+                expd = work.tile([P, 3 * P], F32, name="expd")
+                exp_sum = stats.tile([P, 1], F32, name="exp_sum")
+                nc.scalar.activation(
+                    expd[:, :width], scores[:, :width], EXP, bias=neg_max[:], scale=1.0, accum_out=exp_sum[:]
+                )
+                inv_sum = stats.tile([P, 1], F32, name="inv_sum")
+                nc.vector.reciprocal(inv_sum[:], exp_sum[:])
+                prob = work.tile([P, 3 * P], BF16, name="prob")
+                nc.vector.tensor_scalar_mul(prob[:, :width], expd[:, :width], inv_sum[:])
+
+                probT_ps = flipped.tile([P, 3 * P], BF16, name="probT_ps", tag="flipped")
+                for i in range(len(key_blocks)):
+                    nc.tensor.transpose(probT_ps[:, i * P : (i + 1) * P], prob[:, i * P : (i + 1) * P], ident[:])
+                probT = work.tile([P, 3 * P], BF16, name="probT")
+                nc.scalar.copy(probT[:, :width], probT_ps[:, :width])
+
+                for i, key_block in enumerate(key_blocks):
+                    nc.tensor.matmul(
+                        out_ps[:, b * P : (b + 1) * P],
+                        vT[:, key_block * P : (key_block + 1) * P],
+                        probT[:, i * P : (i + 1) * P],
+                        start=(i == 0),
+                        stop=(i == len(key_blocks) - 1),
+                    )
+
+            cols = slice(piece * PIECE, (piece + 1) * PIECE)
+            nc.vector.tensor_copy(out_sb[:, cols], out_ps[:])
+            nc.sync.dma_start(out[:, cols], out_sb[:, cols])

@@ -16,6 +16,7 @@ PIECE = 512
 N_PIECES = N // PIECE
 N_BLOCKS = N // P
 BLOCKS_PER_PIECE = PIECE // P
+WARM_UP_MATMULS = 4
 MASKED = -1.0e30
 
 PAIRS_IN_BAND = N * (2 * W + 1) - W * (W + 1)
@@ -54,6 +55,12 @@ def tile_longformerselfattention_kernel(tc, table, wq, wk, wv, bq, bv, offs, out
         warm = stats.tile([P, 1], F32, name="warm")
         nc.vector.memset(warm[:], 0.0)
         nc.scalar.activation(warm[:], warm[:], EXP)
+
+        zeros = held.tile([P, PIECE], BF16, name="zeros")
+        nc.vector.memset(zeros[:], 0.0)
+        unread = sums.tile([P, PIECE], F32, name="unread", tag="out_ps")
+        for repeat in range(WARM_UP_MATMULS):
+            nc.tensor.matmul(unread[:], zeros[:, :P], zeros[:], start=True, stop=True)
 
         ident = held.tile([P, P], BF16, name="ident")
         make_identity(nc, ident[:])

@@ -16,7 +16,7 @@ PIECE = 512
 N_PIECES = N // PIECE
 N_BLOCKS = N // P
 BLOCKS_PER_PIECE = PIECE // P
-WARM_UP_MATMULS = 4
+WARM_UP_MATMULS = 16
 MASKED = -1.0e30
 
 PAIRS_IN_BAND = N * (2 * W + 1) - W * (W + 1)
@@ -28,12 +28,18 @@ def tile_longformerselfattention_kernel(tc, table, wq, wk, wv, bq, bv, offs, out
     with (
         tc.tile_pool(name="lists", bufs=1) as lists,
         tc.tile_pool(name="held", bufs=1) as held,
-        tc.tile_pool(name="work", bufs=3) as work,
-        tc.tile_pool(name="stats", bufs=4) as stats,
+        tc.tile_pool(name="work", bufs=6) as work,
+        tc.tile_pool(name="stats", bufs=8) as stats,
         tc.psum_pool(name="products", bufs=4) as products,
         tc.psum_pool(name="flipped", bufs=2) as flipped,
         tc.psum_pool(name="sums", bufs=2) as sums,
     ):
+        zeros = held.tile([P, P], BF16, name="zeros")
+        nc.gpsimd.memset(zeros[:], 0.0)
+        unread = sums.tile([P, P], F32, name="unread", tag="out_ps")
+        for repeat in range(WARM_UP_MATMULS):
+            nc.tensor.matmul(unread[:], zeros[:], zeros[:], start=True, stop=True)
+
         table_rows = held.tile([P, V // P, E], BF16, name="table_rows")
         table_view = table.rearrange("(r p) d -> p r d", p=P)
         nc.sync.dma_start(table_rows[:, 0:2, :], table_view[:, 0:2, :])
@@ -56,12 +62,6 @@ def tile_longformerselfattention_kernel(tc, table, wq, wk, wv, bq, bv, offs, out
         nc.vector.memset(warm[:], 0.0)
         nc.scalar.activation(warm[:], warm[:], EXP)
 
-        zeros = held.tile([P, PIECE], BF16, name="zeros")
-        nc.vector.memset(zeros[:], 0.0)
-        unread = sums.tile([P, PIECE], F32, name="unread", tag="out_ps")
-        for repeat in range(WARM_UP_MATMULS):
-            nc.tensor.matmul(unread[:], zeros[:, :P], zeros[:], start=True, stop=True)
-
         ident = held.tile([P, P], BF16, name="ident")
         make_identity(nc, ident[:])
         distance = held.tile([P, 3 * P], I32, name="distance")
@@ -80,6 +80,7 @@ def tile_longformerselfattention_kernel(tc, table, wq, wk, wv, bq, bv, offs, out
         q_sb = held.tile([E, N], BF16, name="q_sb")
         key_sb = held.tile([E, N], BF16, name="key_sb")
         v_sb = held.tile([E, N], BF16, name="v_sb")
+
         def project(weights, piece):
             looked_up = tableT[:].indirect(offsets[:, piece * (PIECE // 16) : (piece + 1) * (PIECE // 16)])
             product = products.tile([E, PIECE], F32, name="product", tag="product")
@@ -104,55 +105,52 @@ def tile_longformerselfattention_kernel(tc, table, wq, wk, wv, bq, bv, offs, out
                 nc.tensor.transpose(vT_ps[:, b * P : (b + 1) * P], v_sb[:, block * P : (block + 1) * P], ident[:])
             nc.vector.tensor_copy(vT[:, piece * PIECE : (piece + 1) * PIECE], vT_ps[:])
 
-        out_sb = held.tile([E, N], F32, name="out_sb")
-        for piece in range(N_PIECES):
-            out_ps = sums.tile([E, PIECE], F32, name="out_ps", tag="out_ps")
-            for b in range(BLOCKS_PER_PIECE):
-                block = piece * BLOCKS_PER_PIECE + b
-                first, last = max(block - 1, 0), min(block + 1, N_BLOCKS - 1)
-                key_blocks = list(range(first, last + 1))
-                width = len(key_blocks) * P
-                mask_from = (first - (block - 1)) * P
+        for block in range(N_BLOCKS):
+            first, last = max(block - 1, 0), min(block + 1, N_BLOCKS - 1)
+            key_blocks = list(range(first, last + 1))
+            width = len(key_blocks) * P
+            mask_from = (first - (block - 1)) * P
 
-                scores = products.tile([P, 3 * P], F32, name="scores", tag="product")
+            scores = products.tile([P, 3 * P], F32, name="scores", tag="product")
+            nc.tensor.matmul(
+                scores[:, :width],
+                q_sb[:, block * P : (block + 1) * P],
+                key_sb[:, first * P : (last + 1) * P],
+                start=True,
+                stop=False,
+            )
+            nc.tensor.matmul(
+                scores[:, :width], ident[:], band_mask[:, mask_from : mask_from + width], start=False, stop=True
+            )
+
+            neg_max = stats.tile([P, 1], F32, name="neg_max")
+            nc.vector.reduce_max(neg_max[:], scores[:, :width], axis=ALONG_FREE, negate=True)
+            expd = work.tile([P, 3 * P], F32, name="expd")
+            exp_sum = stats.tile([P, 1], F32, name="exp_sum")
+            nc.scalar.activation(
+                expd[:, :width], scores[:, :width], EXP, bias=neg_max[:], scale=1.0, accum_out=exp_sum[:]
+            )
+            inv_sum = stats.tile([P, 1], F32, name="inv_sum")
+            nc.vector.reciprocal(inv_sum[:], exp_sum[:])
+            prob = work.tile([P, 3 * P], BF16, name="prob")
+            nc.vector.tensor_scalar_mul(prob[:, :width], expd[:, :width], inv_sum[:])
+
+            probT_ps = flipped.tile([P, 3 * P], BF16, name="probT_ps", tag="flipped")
+            for i in range(len(key_blocks)):
+                nc.tensor.transpose(probT_ps[:, i * P : (i + 1) * P], prob[:, i * P : (i + 1) * P], ident[:])
+            probT = work.tile([P, 3 * P], BF16, name="probT")
+            nc.scalar.copy(probT[:, :width], probT_ps[:, :width])
+
+            out_ps = sums.tile([E, P], F32, name="out_ps", tag="out_ps")
+            for i, key_block in enumerate(key_blocks):
                 nc.tensor.matmul(
-                    scores[:, :width],
-                    q_sb[:, block * P : (block + 1) * P],
-                    key_sb[:, first * P : (last + 1) * P],
-                    start=True,
-                    stop=False,
-                )
-                nc.tensor.matmul(
-                    scores[:, :width], ident[:], band_mask[:, mask_from : mask_from + width], start=False, stop=True
+                    out_ps[:],
+                    vT[:, key_block * P : (key_block + 1) * P],
+                    probT[:, i * P : (i + 1) * P],
+                    start=(i == 0),
+                    stop=(i == len(key_blocks) - 1),
                 )
 
-                neg_max = stats.tile([P, 1], F32, name="neg_max")
-                nc.vector.reduce_max(neg_max[:], scores[:, :width], axis=ALONG_FREE, negate=True)
-                expd = work.tile([P, 3 * P], F32, name="expd")
-                exp_sum = stats.tile([P, 1], F32, name="exp_sum")
-                nc.scalar.activation(
-                    expd[:, :width], scores[:, :width], EXP, bias=neg_max[:], scale=1.0, accum_out=exp_sum[:]
-                )
-                inv_sum = stats.tile([P, 1], F32, name="inv_sum")
-                nc.vector.reciprocal(inv_sum[:], exp_sum[:])
-                prob = work.tile([P, 3 * P], BF16, name="prob")
-                nc.vector.tensor_scalar_mul(prob[:, :width], expd[:, :width], inv_sum[:])
-
-                probT_ps = flipped.tile([P, 3 * P], BF16, name="probT_ps", tag="flipped")
-                for i in range(len(key_blocks)):
-                    nc.tensor.transpose(probT_ps[:, i * P : (i + 1) * P], prob[:, i * P : (i + 1) * P], ident[:])
-                probT = work.tile([P, 3 * P], BF16, name="probT")
-                nc.scalar.copy(probT[:, :width], probT_ps[:, :width])
-
-                for i, key_block in enumerate(key_blocks):
-                    nc.tensor.matmul(
-                        out_ps[:, b * P : (b + 1) * P],
-                        vT[:, key_block * P : (key_block + 1) * P],
-                        probT[:, i * P : (i + 1) * P],
-                        start=(i == 0),
-                        stop=(i == len(key_blocks) - 1),
-                    )
-
-            cols = slice(piece * PIECE, (piece + 1) * PIECE)
-            nc.vector.tensor_copy(out_sb[:, cols], out_ps[:])
-            nc.sync.dma_start(out[:, cols], out_sb[:, cols])
+            out_sb = work.tile([E, P], F32, name="out_sb")
+            nc.vector.tensor_copy(out_sb[:], out_ps[:])
+            nc.sync.dma_start(out[:, block * P : (block + 1) * P], out_sb[:])

@@ -16,7 +16,6 @@ PIECE = 512
 N_PIECES = N // PIECE
 N_BLOCKS = N // P
 BLOCKS_PER_PIECE = PIECE // P
-WARM_UP_MATMULS = 16
 MASKED = -1.0e30
 
 PAIRS_IN_BAND = N * (2 * W + 1) - W * (W + 1)
@@ -34,12 +33,6 @@ def tile_longformerselfattention_kernel(tc, table, wq, wk, wv, bq, bv, offs, out
         tc.psum_pool(name="flipped", bufs=2) as flipped,
         tc.psum_pool(name="sums", bufs=2) as sums,
     ):
-        zeros = held.tile([P, P], BF16, name="zeros")
-        nc.gpsimd.memset(zeros[:], 0.0)
-        unread = sums.tile([P, P], F32, name="unread", tag="out_ps")
-        for repeat in range(WARM_UP_MATMULS):
-            nc.tensor.matmul(unread[:], zeros[:], zeros[:], start=True, stop=True)
-
         table_rows = held.tile([P, V // P, E], BF16, name="table_rows")
         table_view = table.rearrange("(r p) d -> p r d", p=P)
         nc.sync.dma_start(table_rows[:, 0:2, :], table_view[:, 0:2, :])
@@ -141,7 +134,7 @@ def tile_longformerselfattention_kernel(tc, table, wq, wk, wv, bq, bv, offs, out
             probT = work.tile([P, 3 * P], BF16, name="probT")
             nc.scalar.copy(probT[:, :width], probT_ps[:, :width])
 
-            out_ps = sums.tile([E, P], F32, name="out_ps", tag="out_ps")
+            out_ps = sums.tile([E, P], F32, name="out_ps")
             for i, key_block in enumerate(key_blocks):
                 nc.tensor.matmul(
                     out_ps[:],

@@ -16,6 +16,8 @@ PIECE = 512
 N_PIECES = N // PIECE
 N_BLOCKS = N // P
 BLOCKS_PER_PIECE = PIECE // P
+WARM_UP_MATMULS = 16
+KEEP_WARM_ROUNDS = 2
 MASKED = -1.0e30
 
 PAIRS_IN_BAND = N * (2 * W + 1) - W * (W + 1)
@@ -33,6 +35,12 @@ def tile_longformerselfattention_kernel(tc, table, wq, wk, wv, bq, bv, offs, out
         tc.psum_pool(name="flipped", bufs=2) as flipped,
         tc.psum_pool(name="sums", bufs=2) as sums,
     ):
+        zeros = held.tile([P, P], BF16, name="zeros")
+        nc.gpsimd.memset(zeros[:], 0.0)
+        unread = sums.tile([P, P], F32, name="unread", tag="out_ps")
+        for repeat in range(WARM_UP_MATMULS):
+            nc.tensor.matmul(unread[:], zeros[:], zeros[:], start=True, stop=True)
+
         table_rows = held.tile([P, V // P, E], BF16, name="table_rows")
         table_view = table.rearrange("(r p) d -> p r d", p=P)
         nc.sync.dma_start(table_rows[:, 0:2, :], table_view[:, 0:2, :])
@@ -69,6 +77,9 @@ def tile_longformerselfattention_kernel(tc, table, wq, wk, wv, bq, bv, offs, out
             nc.tensor.transpose(tableT_ps[:, r * P : (r + 1) * P], table_rows[:, r, :], ident[:])
         tableT = held.tile([E, V], BF16, name="tableT")
         nc.vector.tensor_copy(tableT[:], tableT_ps[:])
+        for repeat in range(KEEP_WARM_ROUNDS):
+            for r in range(V // P):
+                nc.tensor.matmul(unread[:], ident[:], table_rows[:, r, :], start=True, stop=True)
 
         q_sb = held.tile([E, N], BF16, name="q_sb")
         key_sb = held.tile([E, N], BF16, name="key_sb")
@@ -134,7 +145,7 @@ def tile_longformerselfattention_kernel(tc, table, wq, wk, wv, bq, bv, offs, out
             probT = work.tile([P, 3 * P], BF16, name="probT")
             nc.scalar.copy(probT[:, :width], probT_ps[:, :width])
 
-            out_ps = sums.tile([E, P], F32, name="out_ps")
+            out_ps = sums.tile([E, P], F32, name="out_ps", tag="out_ps")
             for i, key_block in enumerate(key_blocks):
                 nc.tensor.matmul(
                     out_ps[:],

@@ -16,8 +16,6 @@ PIECE = 512
 N_PIECES = N // PIECE
 N_BLOCKS = N // P
 BLOCKS_PER_PIECE = PIECE // P
-WARM_UP_MATMULS = 16
-KEEP_WARM_ROUNDS = 2
 MASKED = -1.0e30
 
 PAIRS_IN_BAND = N * (2 * W + 1) - W * (W + 1)
@@ -35,28 +33,23 @@ def tile_longformerselfattention_kernel(tc, table, wq, wk, wv, bq, bv, offs, out
         tc.psum_pool(name="flipped", bufs=2) as flipped,
         tc.psum_pool(name="sums", bufs=2) as sums,
     ):
-        zeros = held.tile([P, P], BF16, name="zeros")
-        nc.gpsimd.memset(zeros[:], 0.0)
-        unread = sums.tile([P, P], F32, name="unread", tag="out_ps")
-        for repeat in range(WARM_UP_MATMULS):
-            nc.tensor.matmul(unread[:], zeros[:], zeros[:], start=True, stop=True)
-
         table_rows = held.tile([P, V // P, E], BF16, name="table_rows")
         table_view = table.rearrange("(r p) d -> p r d", p=P)
-        nc.sync.dma_start(table_rows[:, 0:2, :], table_view[:, 0:2, :])
-        nc.scalar.dma_start(table_rows[:, 2:4, :], table_view[:, 2:4, :])
         offsets = lists.tile([P, N // 16], U16, name="offsets")
-        nc.sync.dma_start(offsets[:], offs)
         wq_sb = held.tile([E, E], BF16, name="wq_sb")
         wk_sb = held.tile([E, E], BF16, name="wk_sb")
         wv_sb = held.tile([E, E], BF16, name="wv_sb")
-        nc.scalar.dma_start(wq_sb[:], wq)
-        nc.sync.dma_start(wk_sb[:], wk)
-        nc.scalar.dma_start(wv_sb[:], wv)
         bq_sb = held.tile([E, 1], F32, name="bq_sb")
         bv_sb = held.tile([E, 1], F32, name="bv_sb")
+        nc.sync.dma_start(table_rows[:, 0:2, :], table_view[:, 0:2, :])
+        nc.scalar.dma_start(table_rows[:, 2:4, :], table_view[:, 2:4, :])
+        nc.sync.dma_start(offsets[:], offs)
+        nc.scalar.dma_start(wk_sb[:], wk)
         with nc.allow_non_contiguous_dma(reason="one float32 of a bias to each partition"):
             nc.sync.dma_start(bq_sb[:], bq)
+        nc.scalar.dma_start(wq_sb[:], wq)
+        nc.sync.dma_start(wv_sb[:], wv)
+        with nc.allow_non_contiguous_dma(reason="one float32 of a bias to each partition"):
             nc.scalar.dma_start(bv_sb[:], bv)
 
         warm = stats.tile([P, 1], F32, name="warm")
@@ -77,9 +70,6 @@ def tile_longformerselfattention_kernel(tc, table, wq, wk, wv, bq, bv, offs, out
             nc.tensor.transpose(tableT_ps[:, r * P : (r + 1) * P], table_rows[:, r, :], ident[:])
         tableT = held.tile([E, V], BF16, name="tableT")
         nc.vector.tensor_copy(tableT[:], tableT_ps[:])
-        for repeat in range(KEEP_WARM_ROUNDS):
-            for r in range(V // P):
-                nc.tensor.matmul(unread[:], ident[:], table_rows[:, r, :], start=True, stop=True)
 
         q_sb = held.tile([E, N], BF16, name="q_sb")
         key_sb = held.tile([E, N], BF16, name="key_sb")
@@ -93,11 +83,11 @@ def tile_longformerselfattention_kernel(tc, table, wq, wk, wv, bq, bv, offs, out
 
         pieces = [slice(piece * PIECE, (piece + 1) * PIECE) for piece in range(N_PIECES)]
         for piece, cols in enumerate(pieces):
+            nc.scalar.copy(key_sb[:, cols], project(wk_sb, piece)[:])
+        for piece, cols in enumerate(pieces):
             nc.vector.tensor_scalar(
                 q_sb[:, cols], project(wq_sb, piece)[:], bq_sb[:], 1.0 / math.sqrt(E), op0=ADD, op1=MULT
             )
-        for piece, cols in enumerate(pieces):
-            nc.scalar.copy(key_sb[:, cols], project(wk_sb, piece)[:])
         for piece, cols in enumerate(pieces):
             nc.scalar.activation(v_sb[:, cols], project(wv_sb, piece)[:], IDENTITY, bias=bv_sb[:], scale=1.0)
 
@@ -145,7 +135,7 @@ def tile_longformerselfattention_kernel(tc, table, wq, wk, wv, bq, bv, offs, out
             probT = work.tile([P, 3 * P], BF16, name="probT")
             nc.scalar.copy(probT[:, :width], probT_ps[:, :width])
 
-            out_ps = sums.tile([E, P], F32, name="out_ps", tag="out_ps")
+            out_ps = sums.tile([E, P], F32, name="out_ps")
             for i, key_block in enumerate(key_blocks):
                 nc.tensor.matmul(
                     out_ps[:],

@@ -103,7 +103,7 @@ def tile_longformerselfattention_kernel(tc, table, wq, wk, wv, bq, bv, offs, out
             first, last = max(block - 1, 0), min(block + 1, N_BLOCKS - 1)
             key_blocks = list(range(first, last + 1))
             width = len(key_blocks) * P
-            mask_from = (first - (block - 1)) * P
+            neighbours = [key_block for key_block in key_blocks if key_block != block]
 
             scores = products.tile([P, 3 * P], F32, name="scores", tag="product")
             nc.tensor.matmul(
@@ -113,9 +113,15 @@ def tile_longformerselfattention_kernel(tc, table, wq, wk, wv, bq, bv, offs, out
                 start=True,
                 stop=False,
             )
-            nc.tensor.matmul(
-                scores[:, :width], ident[:], band_mask[:, mask_from : mask_from + width], start=False, stop=True
-            )
+            for key_block in neighbours:
+                i, side = key_block - first, key_block - block + 1
+                nc.tensor.matmul(
+                    scores[:, i * P : (i + 1) * P],
+                    ident[:],
+                    band_mask[:, side * P : (side + 1) * P],
+                    start=False,
+                    stop=(key_block == neighbours[-1]),
+                )
 
             neg_max = stats.tile([P, 1], F32, name="neg_max")
             nc.vector.reduce_max(neg_max[:], scores[:, :width], axis=ALONG_FREE, negate=True)
@@ -127,13 +133,13 @@ def tile_longformerselfattention_kernel(tc, table, wq, wk, wv, bq, bv, offs, out
             inv_sum = stats.tile([P, 1], F32, name="inv_sum")
             nc.vector.reciprocal(inv_sum[:], exp_sum[:])
             prob = work.tile([P, 3 * P], BF16, name="prob")
-            nc.vector.tensor_scalar_mul(prob[:, :width], expd[:, :width], inv_sum[:])
+            nc.gpsimd.tensor_scalar(prob[:, :width], expd[:, :width], inv_sum[:], 1.0, op0=MULT, op1=MULT)
 
             probT_ps = flipped.tile([P, 3 * P], BF16, name="probT_ps", tag="flipped")
             for i in range(len(key_blocks)):
                 nc.tensor.transpose(probT_ps[:, i * P : (i + 1) * P], prob[:, i * P : (i + 1) * P], ident[:])
             probT = work.tile([P, 3 * P], BF16, name="probT")
-            nc.scalar.copy(probT[:, :width], probT_ps[:, :width])
+            nc.vector.tensor_copy(probT[:, :width], probT_ps[:, :width])
 
             out_ps = sums.tile([E, P], F32, name="out_ps")
             for i, key_block in enumerate(key_blocks):
@@ -146,5 +152,5 @@ def tile_longformerselfattention_kernel(tc, table, wq, wk, wv, bq, bv, offs, out
                 )
 
             out_sb = work.tile([E, P], F32, name="out_sb")
-            nc.vector.tensor_copy(out_sb[:], out_ps[:])
+            nc.scalar.copy(out_sb[:], out_ps[:])
             nc.sync.dma_start(out[:, block * P : (block + 1) * P], out_sb[:])

@@ -103,7 +103,7 @@ def tile_longformerselfattention_kernel(tc, table, wq, wk, wv, bq, bv, offs, out
             first, last = max(block - 1, 0), min(block + 1, N_BLOCKS - 1)
             key_blocks = list(range(first, last + 1))
             width = len(key_blocks) * P
-            neighbours = [key_block for key_block in key_blocks if key_block != block]
+            mask_from = (first - (block - 1)) * P
 
             scores = products.tile([P, 3 * P], F32, name="scores", tag="product")
             nc.tensor.matmul(
@@ -113,15 +113,9 @@ def tile_longformerselfattention_kernel(tc, table, wq, wk, wv, bq, bv, offs, out
                 start=True,
                 stop=False,
             )
-            for key_block in neighbours:
-                i, side = key_block - first, key_block - block + 1
-                nc.tensor.matmul(
-                    scores[:, i * P : (i + 1) * P],
-                    ident[:],
-                    band_mask[:, side * P : (side + 1) * P],
-                    start=False,
-                    stop=(key_block == neighbours[-1]),
-                )
+            nc.tensor.matmul(
+                scores[:, :width], ident[:], band_mask[:, mask_from : mask_from + width], start=False, stop=True
+            )
 
             neg_max = stats.tile([P, 1], F32, name="neg_max")
             nc.vector.reduce_max(neg_max[:], scores[:, :width], axis=ALONG_FREE, negate=True)
@@ -133,7 +127,7 @@ def tile_longformerselfattention_kernel(tc, table, wq, wk, wv, bq, bv, offs, out
             inv_sum = stats.tile([P, 1], F32, name="inv_sum")
             nc.vector.reciprocal(inv_sum[:], exp_sum[:])
             prob = work.tile([P, 3 * P], BF16, name="prob")
-            nc.gpsimd.tensor_scalar(prob[:, :width], expd[:, :width], inv_sum[:], 1.0, op0=MULT, op1=MULT)
+            nc.vector.tensor_scalar_mul(prob[:, :width], expd[:, :width], inv_sum[:])
 
             probT_ps = flipped.tile([P, 3 * P], BF16, name="probT_ps", tag="flipped")
             for i in range(len(key_blocks)):

@@ -99,22 +99,35 @@ def tile_longformerselfattention_kernel(tc, table, wq, wk, wv, bq, bv, offs, out
                 nc.tensor.transpose(vT_ps[:, b * P : (b + 1) * P], v_sb[:, block * P : (block + 1) * P], ident[:])
             nc.vector.tensor_copy(vT[:, piece * PIECE : (piece + 1) * PIECE], vT_ps[:])
 
+        key_by_block = key_sb[:].rearrange("c (k t) -> c k t", t=P)
+        mask_by_block = band_mask[:].rearrange("j (k t) -> j k t", t=P)
         for block in range(N_BLOCKS):
-            first, last = max(block - 1, 0), min(block + 1, N_BLOCKS - 1)
-            key_blocks = list(range(first, last + 1))
+            neighbours = [b for b in (block - 1, block + 1) if 0 <= b < N_BLOCKS]
+            key_blocks = neighbours + [block]
             width = len(key_blocks) * P
-            mask_from = (first - (block - 1)) * P
+            masked = len(neighbours) * P
+            step = 2 if len(neighbours) == 2 else 1
+            thirds = [b - (block - 1) for b in neighbours]
+            q_block = q_sb[:, block * P : (block + 1) * P]
 
             scores = products.tile([P, 3 * P], F32, name="scores", tag="product")
+            scores_by_block = scores[:].rearrange("j (k t) -> j k t", t=P)
             nc.tensor.matmul(
-                scores[:, :width],
-                q_sb[:, block * P : (block + 1) * P],
-                key_sb[:, first * P : (last + 1) * P],
+                scores_by_block[:, : len(neighbours), :],
+                ident[:],
+                mask_by_block[:, thirds[0] : thirds[-1] + 1 : step, :],
                 start=True,
                 stop=False,
             )
             nc.tensor.matmul(
-                scores[:, :width], ident[:], band_mask[:, mask_from : mask_from + width], start=False, stop=True
+                scores_by_block[:, : len(neighbours), :],
+                q_block,
+                key_by_block[:, neighbours[0] : neighbours[-1] + 1 : step, :],
+                start=False,
+                stop=False,
+            )
+            nc.tensor.matmul(
+                scores[:, masked:width], q_block, key_sb[:, block * P : (block + 1) * P], start=False, stop=True
             )
 
             neg_max = stats.tile([P, 1], F32, name="neg_max")

@@ -29,7 +29,7 @@ def tile_longformerselfattention_kernel(tc, table, wq, wk, wv, bq, bv, offs, out
         tc.tile_pool(name="held", bufs=1) as held,
         tc.tile_pool(name="work", bufs=6) as work,
         tc.tile_pool(name="stats", bufs=8) as stats,
-        tc.psum_pool(name="products", bufs=4) as products,
+        tc.psum_pool(name="score_banks", bufs=4) as score_banks,
         tc.psum_pool(name="flipped", bufs=2) as flipped,
         tc.psum_pool(name="sums", bufs=2) as sums,
     ):
@@ -56,14 +56,14 @@ def tile_longformerselfattention_kernel(tc, table, wq, wk, wv, bq, bv, offs, out
         nc.vector.memset(warm[:], 0.0)
         nc.scalar.activation(warm[:], warm[:], EXP)
 
+        distance = held.tile([P, 2 * P], I32, name="distance")
+        nc.gpsimd.iota(distance[:], pattern=[[2 * P, 2], [1, P]], base=-P, channel_multiplier=-1)
+        distance_sq = held.tile([P, 2 * P], F32, name="distance_sq")
+        nc.vector.tensor_tensor(distance_sq[:], distance[:], distance[:], MULT)
+        band_mask = held.tile([P, 2 * P], BF16, name="band_mask")
+        nc.vector.tensor_scalar(band_mask[:], distance_sq[:], float(W * W), MASKED, op0=IS_GT, op1=MULT)
         ident = held.tile([P, P], BF16, name="ident")
         make_identity(nc, ident[:])
-        distance = held.tile([P, 3 * P], I32, name="distance")
-        nc.gpsimd.iota(distance[:], pattern=[[1, 3 * P]], base=-P, channel_multiplier=-1)
-        distance_sq = held.tile([P, 3 * P], F32, name="distance_sq")
-        nc.vector.tensor_tensor(distance_sq[:], distance[:], distance[:], MULT)
-        band_mask = held.tile([P, 3 * P], BF16, name="band_mask")
-        nc.vector.tensor_scalar(band_mask[:], distance_sq[:], float(W * W), MASKED, op0=IS_GT, op1=MULT)
 
         tableT_ps = flipped.tile([E, V], BF16, name="tableT_ps", tag="flipped")
         for r in range(V // P):
@@ -77,7 +77,8 @@ def tile_longformerselfattention_kernel(tc, table, wq, wk, wv, bq, bv, offs, out
 
         def project(weights, piece):
             looked_up = tableT[:].indirect(offsets[:, piece * (PIECE // 16) : (piece + 1) * (PIECE // 16)])
-            product = products.tile([E, PIECE], F32, name="product", tag="product")
+            borrowed, tag = ((flipped, "flipped"), (sums, "sums"))[piece]
+            product = borrowed.tile([E, PIECE], F32, name="product", tag=tag)
             nc.tensor.matmul(product[:], weights[:], looked_up, start=True, stop=True)
             return product
 
@@ -100,24 +101,19 @@ def tile_longformerselfattention_kernel(tc, table, wq, wk, wv, bq, bv, offs, out
             nc.vector.tensor_copy(vT[:, piece * PIECE : (piece + 1) * PIECE], vT_ps[:])
 
         key_by_block = key_sb[:].rearrange("c (k t) -> c k t", t=P)
-        mask_by_block = band_mask[:].rearrange("j (k t) -> j k t", t=P)
         for block in range(N_BLOCKS):
             neighbours = [b for b in (block - 1, block + 1) if 0 <= b < N_BLOCKS]
             key_blocks = neighbours + [block]
             width = len(key_blocks) * P
             masked = len(neighbours) * P
             step = 2 if len(neighbours) == 2 else 1
-            thirds = [b - (block - 1) for b in neighbours]
+            mask_from = 0 if neighbours[0] < block else P
             q_block = q_sb[:, block * P : (block + 1) * P]
 
-            scores = products.tile([P, 3 * P], F32, name="scores", tag="product")
+            scores = score_banks.tile([P, 3 * P], F32, name="scores")
             scores_by_block = scores[:].rearrange("j (k t) -> j k t", t=P)
             nc.tensor.matmul(
-                scores_by_block[:, : len(neighbours), :],
-                ident[:],
-                mask_by_block[:, thirds[0] : thirds[-1] + 1 : step, :],
-                start=True,
-                stop=False,
+                scores[:, :masked], ident[:], band_mask[:, mask_from : mask_from + masked], start=True, stop=False
             )
             nc.tensor.matmul(
                 scores_by_block[:, : len(neighbours), :],
@@ -148,7 +144,7 @@ def tile_longformerselfattention_kernel(tc, table, wq, wk, wv, bq, bv, offs, out
             probT = work.tile([P, 3 * P], BF16, name="probT")
             nc.vector.tensor_copy(probT[:, :width], probT_ps[:, :width])
 
-            out_ps = sums.tile([E, P], F32, name="out_ps")
+            out_ps = sums.tile([E, P], F32, name="out_ps", tag="sums")
             for i, key_block in enumerate(key_blocks):
                 nc.tensor.matmul(
                     out_ps[:],

@@ -1,10 +1,9 @@
 import math
 
 import concourse.mybir as mybir
-from concourse.masks import make_identity
 
 BF16, F32, I32, U16 = mybir.dt.bfloat16, mybir.dt.float32, mybir.dt.int32, mybir.dt.uint16
-ADD, MULT, IS_GT = mybir.AluOpType.add, mybir.AluOpType.mult, mybir.AluOpType.is_gt
+ADD, MULT, IS_GT, IS_EQUAL = mybir.AluOpType.add, mybir.AluOpType.mult, mybir.AluOpType.is_gt, mybir.AluOpType.is_equal
 EXP = mybir.ActivationFunctionType.Exp
 IDENTITY = mybir.ActivationFunctionType.Identity
 ALONG_FREE = mybir.AxisListType.X
@@ -63,7 +62,7 @@ def tile_longformerselfattention_kernel(tc, table, wq, wk, wv, bq, bv, offs, out
         band_mask = held.tile([P, 2 * P], BF16, name="band_mask")
         nc.vector.tensor_scalar(band_mask[:], distance_sq[:], float(W * W), MASKED, op0=IS_GT, op1=MULT)
         ident = held.tile([P, P], BF16, name="ident")
-        make_identity(nc, ident[:])
+        nc.vector.tensor_scalar(ident[:], distance[:, :P], float(-P), None, op0=IS_EQUAL)
 
         tableT_ps = flipped.tile([E, V], BF16, name="tableT_ps", tag="flipped")
         for r in range(V // P):
@@ -136,7 +135,10 @@ def tile_longformerselfattention_kernel(tc, table, wq, wk, wv, bq, bv, offs, out
             inv_sum = stats.tile([P, 1], F32, name="inv_sum")
             nc.vector.reciprocal(inv_sum[:], exp_sum[:])
             prob = work.tile([P, 3 * P], BF16, name="prob")
-            nc.vector.tensor_scalar_mul(prob[:, :width], expd[:, :width], inv_sum[:])
+            if block % 2 == 1:
+                nc.gpsimd.tensor_scalar(prob[:, :width], expd[:, :width], inv_sum[:], 0.0, op0=MULT, op1=ADD)
+            else:
+                nc.vector.tensor_scalar_mul(prob[:, :width], expd[:, :width], inv_sum[:])
 
             probT_ps = flipped.tile([P, 3 * P], BF16, name="probT_ps", tag="flipped")
             for i in range(len(key_blocks)):

@@ -26,6 +26,7 @@ def tile_longformerselfattention_kernel(tc, table, wq, wk, wv, bq, bv, offs, out
     with (
         tc.tile_pool(name="lists", bufs=1) as lists,
         tc.tile_pool(name="held", bufs=1) as held,
+        tc.tile_pool(name="held_per_block", bufs=N_BLOCKS) as held_per_block,
         tc.tile_pool(name="work", bufs=6) as work,
         tc.tile_pool(name="stats", bufs=8) as stats,
         tc.psum_pool(name="score_banks", bufs=4) as score_banks,
@@ -63,6 +64,8 @@ def tile_longformerselfattention_kernel(tc, table, wq, wk, wv, bq, bv, offs, out
         nc.vector.tensor_scalar(band_mask[:], distance_sq[:], float(W * W), MASKED, op0=IS_GT, op1=MULT)
         ident = held.tile([P, P], BF16, name="ident")
         nc.vector.tensor_scalar(ident[:], distance[:, :P], float(-P), None, op0=IS_EQUAL)
+        ident_f32 = held.tile([P, P], F32, name="ident_f32")
+        nc.vector.tensor_copy(ident_f32[:], ident[:])
 
         tableT_ps = flipped.tile([E, V], BF16, name="tableT_ps", tag="flipped")
         for r in range(V // P):
@@ -91,20 +94,17 @@ def tile_longformerselfattention_kernel(tc, table, wq, wk, wv, bq, bv, offs, out
         for piece, cols in enumerate(pieces):
             nc.scalar.activation(v_sb[:, cols], project(wv_sb, piece)[:], IDENTITY, bias=bv_sb[:], scale=1.0)
 
-        vT = held.tile([P, N], BF16, name="vT")
-        for piece in range(N_PIECES):
-            vT_ps = flipped.tile([P, PIECE], BF16, name="vT_ps", tag="flipped")
-            for b in range(BLOCKS_PER_PIECE):
-                block = piece * BLOCKS_PER_PIECE + b
-                nc.tensor.transpose(vT_ps[:, b * P : (b + 1) * P], v_sb[:, block * P : (block + 1) * P], ident[:])
-            nc.vector.tensor_copy(vT[:, piece * PIECE : (piece + 1) * PIECE], vT_ps[:])
-
         key_by_block = key_sb[:].rearrange("c (k t) -> c k t", t=P)
+
+        def neighbours_of(block):
+            return [b for b in (block - 1, block + 1) if 0 <= b < N_BLOCKS]
+
+        probs = []
+        exp_sums = held.tile([P, N_BLOCKS], F32, name="exp_sums")
         for block in range(N_BLOCKS):
-            neighbours = [b for b in (block - 1, block + 1) if 0 <= b < N_BLOCKS]
-            key_blocks = neighbours + [block]
-            width = len(key_blocks) * P
+            neighbours = neighbours_of(block)
             masked = len(neighbours) * P
+            width = masked + P
             step = 2 if len(neighbours) == 2 else 1
             mask_from = 0 if neighbours[0] < block else P
             q_block = q_sb[:, block * P : (block + 1) * P]
@@ -127,35 +127,62 @@ def tile_longformerselfattention_kernel(tc, table, wq, wk, wv, bq, bv, offs, out
 
             neg_max = stats.tile([P, 1], F32, name="neg_max")
             nc.vector.reduce_max(neg_max[:], scores[:, :width], axis=ALONG_FREE, negate=True)
-            expd = work.tile([P, 3 * P], F32, name="expd")
-            exp_sum = stats.tile([P, 1], F32, name="exp_sum")
+            prob = held_per_block.tile([P, 3 * P], BF16, name="prob")
             nc.scalar.activation(
-                expd[:, :width], scores[:, :width], EXP, bias=neg_max[:], scale=1.0, accum_out=exp_sum[:]
+                prob[:, :width], scores[:, :width], EXP, bias=neg_max[:], scale=1.0,
+                accum_out=exp_sums[:, block : block + 1],
             )
-            inv_sum = stats.tile([P, 1], F32, name="inv_sum")
-            nc.vector.reciprocal(inv_sum[:], exp_sum[:])
-            prob = work.tile([P, 3 * P], BF16, name="prob")
-            if block % 2 == 1:
-                nc.gpsimd.tensor_scalar(prob[:, :width], expd[:, :width], inv_sum[:], 0.0, op0=MULT, op1=ADD)
-            else:
-                nc.vector.tensor_scalar_mul(prob[:, :width], expd[:, :width], inv_sum[:])
+            probs.append(prob)
 
-            probT_ps = flipped.tile([P, 3 * P], BF16, name="probT_ps", tag="flipped")
-            for i in range(len(key_blocks)):
-                nc.tensor.transpose(probT_ps[:, i * P : (i + 1) * P], prob[:, i * P : (i + 1) * P], ident[:])
-            probT = work.tile([P, 3 * P], BF16, name="probT")
-            nc.vector.tensor_copy(probT[:, :width], probT_ps[:, :width])
+        vT = held.tile([P, N], BF16, name="vT")
+        for piece in range(N_PIECES):
+            vT_ps = flipped.tile([P, PIECE], BF16, name="vT_ps", tag="flipped")
+            for b in range(BLOCKS_PER_PIECE):
+                block = piece * BLOCKS_PER_PIECE + b
+                nc.tensor.transpose(vT_ps[:, b * P : (b + 1) * P], v_sb[:, block * P : (block + 1) * P], ident[:])
+            nc.vector.tensor_copy(vT[:, piece * PIECE : (piece + 1) * PIECE], vT_ps[:])
 
-            out_ps = sums.tile([E, P], F32, name="out_ps", tag="sums")
-            for i, key_block in enumerate(key_blocks):
-                nc.tensor.matmul(
-                    out_ps[:],
-                    vT[:, key_block * P : (key_block + 1) * P],
-                    probT[:, i * P : (i + 1) * P],
-                    start=(i == 0),
-                    stop=(i == len(key_blocks) - 1),
+        probTs = []
+        inv_sums = held.tile([P, N_BLOCKS], F32, name="inv_sums")
+        divisor = held.tile([E, N], F32, name="divisor")
+        for half, cols in enumerate(pieces):
+            blocks = range(half * BLOCKS_PER_PIECE, (half + 1) * BLOCKS_PER_PIECE)
+
+            nc.vector.reciprocal(inv_sums[:, blocks.start : blocks.stop], exp_sums[:, blocks.start : blocks.stop])
+            divisor_ps = sums.tile([E, PIECE], F32, name="divisor_ps", tag="sums")
+            for b, block in enumerate(blocks):
+                nc.tensor.transpose(
+                    divisor_ps[:, b * P : (b + 1) * P],
+                    inv_sums[:, block : block + 1].to_broadcast([P, E]),
+                    ident_f32[:],
                 )
+            nc.scalar.copy(divisor[:, cols], divisor_ps[:])
 
-            out_sb = work.tile([E, P], F32, name="out_sb")
-            nc.scalar.copy(out_sb[:], out_ps[:])
-            nc.sync.dma_start(out[:, block * P : (block + 1) * P], out_sb[:])
+            for block in blocks:
+                n_keys = len(neighbours_of(block)) + 1
+                pool, tag = ((flipped, "flipped"), (score_banks, "scores"))[half]
+                probT_ps = pool.tile([P, 3 * P], BF16, name="probT_ps", tag=tag)
+                for i in range(n_keys):
+                    nc.tensor.transpose(probT_ps[:, i * P : (i + 1) * P], probs[block][:, i * P : (i + 1) * P], ident[:])
+                probT = held_per_block.tile([P, 3 * P], BF16, name="probT")
+                nc.vector.tensor_copy(probT[:, : n_keys * P], probT_ps[:, : n_keys * P])
+                probTs.append(probT)
+
+        for pair in range(N_BLOCKS // 2):
+            pool, tag = ((flipped, "flipped"), (sums, "sums"))[2 * pair // BLOCKS_PER_PIECE]
+            queries = slice(2 * pair * P, 2 * (pair + 1) * P)
+            out_ps = pool.tile([E, 2 * P], F32, name="out_ps", tag=tag)
+            for side in range(2):
+                block = 2 * pair + side
+                key_blocks = neighbours_of(block) + [block]
+                for i, key_block in enumerate(key_blocks):
+                    nc.tensor.matmul(
+                        out_ps[:, side * P : (side + 1) * P],
+                        vT[:, key_block * P : (key_block + 1) * P],
+                        probTs[block][:, i * P : (i + 1) * P],
+                        start=(i == 0),
+                        stop=(i == len(key_blocks) - 1),
+                    )
+            out_sb = work.tile([E, 2 * P], F32, name="out_sb")
+            nc.vector.tensor_tensor(out_sb[:], out_ps[:], divisor[:, queries], MULT)
+            nc.sync.dma_start(out[:, queries], out_sb[:])

@@ -101,6 +101,29 @@ def tile_longformerselfattention_kernel(tc, table, wq, wk, wv, bq, bv, offs, out
 
         probs = []
         exp_sums = held.tile([P, N_BLOCKS], F32, name="exp_sums")
+        inv_sums = held.tile([P, N_BLOCKS], F32, name="inv_sums")
+        divisor = held.tile([E, N], F32, name="divisor")
+        first, second = range(N_PIECES)
+        divisor_banks = {}
+
+        def invert_sums(half):
+            blocks = slice(half * BLOCKS_PER_PIECE, (half + 1) * BLOCKS_PER_PIECE)
+            nc.vector.reciprocal(inv_sums[:, blocks], exp_sums[:, blocks])
+
+        def flip_sums(half):
+            blocks = range(half * BLOCKS_PER_PIECE, (half + 1) * BLOCKS_PER_PIECE)
+            divisor_ps = sums.tile([E, PIECE], F32, name="divisor_ps", tag="sums")
+            for b, block in enumerate(blocks):
+                nc.tensor.transpose(
+                    divisor_ps[:, b * P : (b + 1) * P],
+                    inv_sums[:, block : block + 1].to_broadcast([P, E]),
+                    ident_f32[:],
+                )
+            divisor_banks[half] = divisor_ps
+
+        def copy_divisors(half):
+            nc.scalar.copy(divisor[:, pieces[half]], divisor_banks[half][:])
+
         for block in range(N_BLOCKS):
             neighbours = neighbours_of(block)
             masked = len(neighbours) * P
@@ -133,40 +156,37 @@ def tile_longformerselfattention_kernel(tc, table, wq, wk, wv, bq, bv, offs, out
                 accum_out=exp_sums[:, block : block + 1],
             )
             probs.append(prob)
+            if block == BLOCKS_PER_PIECE + 1:
+                invert_sums(first)
+                flip_sums(first)
 
         vT = held.tile([P, N], BF16, name="vT")
         for piece in range(N_PIECES):
             vT_ps = flipped.tile([P, PIECE], BF16, name="vT_ps", tag="flipped")
             for b in range(BLOCKS_PER_PIECE):
                 block = piece * BLOCKS_PER_PIECE + b
-                nc.tensor.transpose(vT_ps[:, b * P : (b + 1) * P], v_sb[:, block * P : (block + 1) * P], ident[:])
+                nc.tensor.matmul(vT_ps[:, b * P : (b + 1) * P], v_sb[:, block * P : (block + 1) * P], ident[:], start=True, stop=True)
             nc.vector.tensor_copy(vT[:, piece * PIECE : (piece + 1) * PIECE], vT_ps[:])
 
+        copy_divisors(first)
         probTs = []
-        inv_sums = held.tile([P, N_BLOCKS], F32, name="inv_sums")
-        divisor = held.tile([E, N], F32, name="divisor")
-        for half, cols in enumerate(pieces):
-            blocks = range(half * BLOCKS_PER_PIECE, (half + 1) * BLOCKS_PER_PIECE)
-
-            nc.vector.reciprocal(inv_sums[:, blocks.start : blocks.stop], exp_sums[:, blocks.start : blocks.stop])
-            divisor_ps = sums.tile([E, PIECE], F32, name="divisor_ps", tag="sums")
-            for b, block in enumerate(blocks):
-                nc.tensor.transpose(
-                    divisor_ps[:, b * P : (b + 1) * P],
-                    inv_sums[:, block : block + 1].to_broadcast([P, E]),
-                    ident_f32[:],
-                )
-            nc.scalar.copy(divisor[:, cols], divisor_ps[:])
-
-            for block in blocks:
-                n_keys = len(neighbours_of(block)) + 1
-                pool, tag = ((flipped, "flipped"), (score_banks, "scores"))[half]
-                probT_ps = pool.tile([P, 3 * P], BF16, name="probT_ps", tag=tag)
-                for i in range(n_keys):
-                    nc.tensor.transpose(probT_ps[:, i * P : (i + 1) * P], probs[block][:, i * P : (i + 1) * P], ident[:])
-                probT = held_per_block.tile([P, 3 * P], BF16, name="probT")
+        for block in range(N_BLOCKS):
+            half = block // BLOCKS_PER_PIECE
+            n_keys = len(neighbours_of(block)) + 1
+            pool, tag = ((flipped, "flipped"), (score_banks, "scores"))[half]
+            probT_ps = pool.tile([P, 3 * P], BF16, name="probT_ps", tag=tag)
+            for i in range(n_keys):
+                nc.tensor.matmul(probT_ps[:, i * P : (i + 1) * P], probs[block][:, i * P : (i + 1) * P], ident[:], start=True, stop=True)
+            probT = held_per_block.tile([P, 3 * P], BF16, name="probT")
+            if half == second and block % 2 == 0:
+                nc.scalar.copy(probT[:, : n_keys * P], probT_ps[:, : n_keys * P])
+            else:
                 nc.vector.tensor_copy(probT[:, : n_keys * P], probT_ps[:, : n_keys * P])
-                probTs.append(probT)
+            probTs.append(probT)
+            if block == N_BLOCKS - 3:
+                invert_sums(second)
+        flip_sums(second)
+        copy_divisors(second)
 
         for pair in range(N_BLOCKS // 2):
             pool, tag = ((flipped, "flipped"), (sums, "sums"))[2 * pair // BLOCKS_PER_PIECE]

@@ -99,32 +99,29 @@ def tile_longformerselfattention_kernel(tc, table, wq, wk, wv, bq, bv, offs, out
         def neighbours_of(block):
             return [b for b in (block - 1, block + 1) if 0 <= b < N_BLOCKS]
 
-        probs = []
+        probs, probTs = [], []
         exp_sums = held.tile([P, N_BLOCKS], F32, name="exp_sums")
         inv_sums = held.tile([P, N_BLOCKS], F32, name="inv_sums")
         divisor = held.tile([E, N], F32, name="divisor")
-        first, second = range(N_PIECES)
-        divisor_banks = {}
+        out_banks = []
 
-        def invert_sums(half):
-            blocks = slice(half * BLOCKS_PER_PIECE, (half + 1) * BLOCKS_PER_PIECE)
-            nc.vector.reciprocal(inv_sums[:, blocks], exp_sums[:, blocks])
+        def invert_sums(blocks):
+            nc.vector.reciprocal(inv_sums[:, blocks.start : blocks.stop], exp_sums[:, blocks.start : blocks.stop])
 
-        def flip_sums(half):
-            blocks = range(half * BLOCKS_PER_PIECE, (half + 1) * BLOCKS_PER_PIECE)
+        def flip_sums(blocks):
             divisor_ps = sums.tile([E, PIECE], F32, name="divisor_ps", tag="sums")
-            for b, block in enumerate(blocks):
+            for i, block in enumerate(blocks):
                 nc.tensor.transpose(
-                    divisor_ps[:, b * P : (b + 1) * P],
+                    divisor_ps[:, i * P : (i + 1) * P],
                     inv_sums[:, block : block + 1].to_broadcast([P, E]),
                     ident_f32[:],
                 )
-            divisor_banks[half] = divisor_ps
+            return divisor_ps
 
-        def copy_divisors(half):
-            nc.scalar.copy(divisor[:, pieces[half]], divisor_banks[half][:])
+        def copy_divisors(blocks, divisor_ps):
+            nc.scalar.copy(divisor[:, blocks.start * P : blocks.stop * P], divisor_ps[:, : len(blocks) * P])
 
-        for block in range(N_BLOCKS):
+        def exponentials(block):
             neighbours = neighbours_of(block)
             masked = len(neighbours) * P
             width = masked + P
@@ -152,13 +149,67 @@ def tile_longformerselfattention_kernel(tc, table, wq, wk, wv, bq, bv, offs, out
             nc.vector.reduce_max(neg_max[:], scores[:, :width], axis=ALONG_FREE, negate=True)
             prob = held_per_block.tile([P, 3 * P], BF16, name="prob")
             nc.scalar.activation(
-                prob[:, :width], scores[:, :width], EXP, bias=neg_max[:], scale=1.0,
+                prob[:, :width],
+                scores[:, :width],
+                EXP,
+                bias=neg_max[:],
+                scale=1.0,
                 accum_out=exp_sums[:, block : block + 1],
             )
             probs.append(prob)
-            if block == BLOCKS_PER_PIECE + 1:
-                invert_sums(first)
-                flip_sums(first)
+
+        def flip(pair):
+            left, right = 2 * pair, 2 * pair + 1
+            parts = [(left, left), (right, left), (left, right), (right, right)]
+            parts += [(left, left - 1)] if left > 0 else []
+            parts += [(right, right + 1)] if right < N_BLOCKS - 1 else []
+            pool, tag = ((flipped, "flipped"), (score_banks, "scores"))[2 * pair // BLOCKS_PER_PIECE]
+            probT_ps = pool.tile([P, 6 * P], BF16, name="probT_ps", tag=tag)
+            for i, (block, key_block) in enumerate(parts):
+                k = (neighbours_of(block) + [block]).index(key_block)
+                nc.tensor.matmul(
+                    probT_ps[:, i * P : (i + 1) * P],
+                    probs[block][:, k * P : (k + 1) * P],
+                    ident[:],
+                    start=True,
+                    stop=True,
+                )
+            probT = held_per_block.tile([P, 6 * P], BF16, name="probT")
+            nc.vector.tensor_copy(probT[:, : len(parts) * P], probT_ps[:, : len(parts) * P])
+            probTs.append(probT)
+
+        def product(pair):
+            left, right = 2 * pair, 2 * pair + 1
+            terms = [(left, slice(0, 2 * P)), (right, slice(0, 2 * P))]
+            terms += [(left - 1, slice(0, P))] if left > 0 else []
+            terms += [(right + 1, slice(P, 2 * P))] if right < N_BLOCKS - 1 else []
+            pool, tag = ((flipped, "flipped"), (score_banks, "scores"))[2 * pair // BLOCKS_PER_PIECE]
+            out_ps = pool.tile([E, 2 * P], F32, name="out_ps", tag=tag)
+            done = 0
+            for i, (key_block, queries) in enumerate(terms):
+                width = queries.stop - queries.start
+                nc.tensor.matmul(
+                    out_ps[:, queries],
+                    vT[:, key_block * P : (key_block + 1) * P],
+                    probTs[pair][:, done : done + width],
+                    start=(i == 0),
+                    stop=(i == len(terms) - 1),
+                )
+                done += width
+            out_banks.append(out_ps)
+
+        def divide(pair):
+            queries = slice(2 * pair * P, 2 * (pair + 1) * P)
+            out_sb = work.tile([E, 2 * P], F32, name="out_sb")
+            nc.vector.tensor_tensor(out_sb[:], out_banks[pair][:], divisor[:, queries], MULT)
+            nc.sync.dma_start(out[:, queries], out_sb[:])
+
+        first_half, third_pair, last_pair = range(0, 4), range(4, 6), range(6, 8)
+        for block in range(N_BLOCKS):
+            exponentials(block)
+            if block == 5:
+                invert_sums(first_half)
+                first_half_ps = flip_sums(first_half)
 
         vT = held.tile([P, N], BF16, name="vT")
         for piece in range(N_PIECES):
@@ -168,41 +219,19 @@ def tile_longformerselfattention_kernel(tc, table, wq, wk, wv, bq, bv, offs, out
                 nc.tensor.matmul(vT_ps[:, b * P : (b + 1) * P], v_sb[:, block * P : (block + 1) * P], ident[:], start=True, stop=True)
             nc.vector.tensor_copy(vT[:, piece * PIECE : (piece + 1) * PIECE], vT_ps[:])
 
-        copy_divisors(first)
-        probTs = []
-        for block in range(N_BLOCKS):
-            half = block // BLOCKS_PER_PIECE
-            n_keys = len(neighbours_of(block)) + 1
-            pool, tag = ((flipped, "flipped"), (score_banks, "scores"))[half]
-            probT_ps = pool.tile([P, 3 * P], BF16, name="probT_ps", tag=tag)
-            for i in range(n_keys):
-                nc.tensor.matmul(probT_ps[:, i * P : (i + 1) * P], probs[block][:, i * P : (i + 1) * P], ident[:], start=True, stop=True)
-            probT = held_per_block.tile([P, 3 * P], BF16, name="probT")
-            if half == second and block % 2 == 0:
-                nc.scalar.copy(probT[:, : n_keys * P], probT_ps[:, : n_keys * P])
-            else:
-                nc.vector.tensor_copy(probT[:, : n_keys * P], probT_ps[:, : n_keys * P])
-            probTs.append(probT)
-            if block == N_BLOCKS - 3:
-                invert_sums(second)
-        flip_sums(second)
-        copy_divisors(second)
-
+        invert_sums(third_pair)
+        third_pair_ps = flip_sums(third_pair)
+        copy_divisors(first_half, first_half_ps)
+        copy_divisors(third_pair, third_pair_ps)
+        flip(0)
+        flip(1)
+        flip(2)
+        invert_sums(last_pair)
+        product(0)
+        flip(3)
+        last_pair_ps = flip_sums(last_pair)
+        copy_divisors(last_pair, last_pair_ps)
+        for pair in (1, 2, 3):
+            product(pair)
         for pair in range(N_BLOCKS // 2):
-            pool, tag = ((flipped, "flipped"), (sums, "sums"))[2 * pair // BLOCKS_PER_PIECE]
-            queries = slice(2 * pair * P, 2 * (pair + 1) * P)
-            out_ps = pool.tile([E, 2 * P], F32, name="out_ps", tag=tag)
-            for side in range(2):
-                block = 2 * pair + side
-                key_blocks = neighbours_of(block) + [block]
-                for i, key_block in enumerate(key_blocks):
-                    nc.tensor.matmul(
-                        out_ps[:, side * P : (side + 1) * P],
-                        vT[:, key_block * P : (key_block + 1) * P],
-                        probTs[block][:, i * P : (i + 1) * P],
-                        start=(i == 0),
-                        stop=(i == len(key_blocks) - 1),
-                    )
-            out_sb = work.tile([E, 2 * P], F32, name="out_sb")
-            nc.vector.tensor_tensor(out_sb[:], out_ps[:], divisor[:, queries], MULT)
-            nc.sync.dma_start(out[:, queries], out_sb[:])
+            divide(pair)

@@ -209,7 +209,6 @@ def tile_longformerselfattention_kernel(tc, table, wq, wk, wv, bq, bv, offs, out
             exponentials(block)
             if block == 5:
                 invert_sums(first_half)
-                first_half_ps = flip_sums(first_half)
 
         vT = held.tile([P, N], BF16, name="vT")
         for piece in range(N_PIECES):
@@ -220,18 +219,21 @@ def tile_longformerselfattention_kernel(tc, table, wq, wk, wv, bq, bv, offs, out
             nc.vector.tensor_copy(vT[:, piece * PIECE : (piece + 1) * PIECE], vT_ps[:])
 
         invert_sums(third_pair)
-        third_pair_ps = flip_sums(third_pair)
-        copy_divisors(first_half, first_half_ps)
-        copy_divisors(third_pair, third_pair_ps)
         flip(0)
         flip(1)
+        first_half_ps = flip_sums(first_half)
+        copy_divisors(first_half, first_half_ps)
         flip(2)
-        invert_sums(last_pair)
         product(0)
+        third_pair_ps = flip_sums(third_pair)
+        copy_divisors(third_pair, third_pair_ps)
+        divide(0)
+        invert_sums(last_pair)
         flip(3)
+        product(1)
         last_pair_ps = flip_sums(last_pair)
         copy_divisors(last_pair, last_pair_ps)
+        product(2)
+        product(3)
         for pair in (1, 2, 3):
-            product(pair)
-        for pair in range(N_BLOCKS // 2):
             divide(pair)

@@ -99,17 +99,15 @@ def tile_longformerselfattention_kernel(tc, table, wq, wk, wv, bq, bv, offs, out
         def neighbours_of(block):
             return [b for b in (block - 1, block + 1) if 0 <= b < N_BLOCKS]
 
-        probs, probTs = [], []
+        probs, probTs, out_banks = [], {}, {}
         exp_sums = held.tile([P, N_BLOCKS], F32, name="exp_sums")
         inv_sums = held.tile([P, N_BLOCKS], F32, name="inv_sums")
         divisor = held.tile([E, N], F32, name="divisor")
-        out_banks = []
-
         def invert_sums(blocks):
             nc.vector.reciprocal(inv_sums[:, blocks.start : blocks.stop], exp_sums[:, blocks.start : blocks.stop])
 
         def flip_sums(blocks):
-            divisor_ps = sums.tile([E, PIECE], F32, name="divisor_ps", tag="sums")
+            divisor_ps = flipped.tile([E, PIECE], F32, name="divisor_ps", tag="flipped")
             for i, block in enumerate(blocks):
                 nc.tensor.transpose(
                     divisor_ps[:, i * P : (i + 1) * P],
@@ -158,57 +156,60 @@ def tile_longformerselfattention_kernel(tc, table, wq, wk, wv, bq, bv, offs, out
             )
             probs.append(prob)
 
-        def flip(pair):
-            left, right = 2 * pair, 2 * pair + 1
-            parts = [(left, left), (right, left), (left, right), (right, right)]
-            parts += [(left, left - 1)] if left > 0 else []
-            parts += [(right, right + 1)] if right < N_BLOCKS - 1 else []
-            pool, tag = ((flipped, "flipped"), (score_banks, "scores"))[2 * pair // BLOCKS_PER_PIECE]
-            probT_ps = pool.tile([P, 6 * P], BF16, name="probT_ps", tag=tag)
-            for i, (block, key_block) in enumerate(parts):
-                k = (neighbours_of(block) + [block]).index(key_block)
-                nc.tensor.matmul(
-                    probT_ps[:, i * P : (i + 1) * P],
-                    probs[block][:, k * P : (k + 1) * P],
-                    ident[:],
-                    start=True,
-                    stop=True,
-                )
-            probT = held_per_block.tile([P, 6 * P], BF16, name="probT")
-            nc.vector.tensor_copy(probT[:, : len(parts) * P], probT_ps[:, : len(parts) * P])
-            probTs.append(probT)
+        def keys_of(group):
+            seen = {}
+            for block in group:
+                for key_block in neighbours_of(block) + [block]:
+                    seen.setdefault(key_block, []).append(block)
+            return sorted(seen.items(), key=lambda item: -len(item[1]))
 
-        def product(pair):
-            left, right = 2 * pair, 2 * pair + 1
-            terms = [(left, slice(0, 2 * P)), (right, slice(0, 2 * P))]
-            terms += [(left - 1, slice(0, P))] if left > 0 else []
-            terms += [(right + 1, slice(P, 2 * P))] if right < N_BLOCKS - 1 else []
-            pool, tag = ((flipped, "flipped"), (score_banks, "scores"))[2 * pair // BLOCKS_PER_PIECE]
-            out_ps = pool.tile([E, 2 * P], F32, name="out_ps", tag=tag)
+        def flip(group):
+            pool, tag = (sums, "sums") if group.stop <= BLOCKS_PER_PIECE else (score_banks, "scores")
+            probT_ps = pool.tile([P, 6 * P], BF16, name="probT_ps", tag=tag)
             done = 0
-            for i, (key_block, queries) in enumerate(terms):
-                width = queries.stop - queries.start
+            for key_block, blocks in keys_of(group):
+                for block in blocks:
+                    k = (neighbours_of(block) + [block]).index(key_block)
+                    nc.tensor.matmul(
+                        probT_ps[:, done : done + P],
+                        probs[block][:, k * P : (k + 1) * P],
+                        ident[:],
+                        start=True,
+                        stop=True,
+                    )
+                    done += P
+            probT = held_per_block.tile([P, 6 * P], BF16, name="probT")
+            nc.vector.tensor_copy(probT[:, :done], probT_ps[:, :done])
+            probTs[group] = probT
+
+        def product(group):
+            pool, tag = (sums, "sums") if group.stop <= BLOCKS_PER_PIECE else (score_banks, "scores")
+            out_ps = pool.tile([E, len(group) * P], F32, name="out_ps", tag=tag)
+            done = 0
+            terms = keys_of(group)
+            for i, (key_block, blocks) in enumerate(terms):
+                first_query = (blocks[0] - group.start) * P
+                width = len(blocks) * P
                 nc.tensor.matmul(
-                    out_ps[:, queries],
+                    out_ps[:, first_query : first_query + width],
                     vT[:, key_block * P : (key_block + 1) * P],
-                    probTs[pair][:, done : done + width],
+                    probTs[group][:, done : done + width],
                     start=(i == 0),
                     stop=(i == len(terms) - 1),
                 )
                 done += width
-            out_banks.append(out_ps)
+            out_banks[group] = out_ps
 
-        def divide(pair):
-            queries = slice(2 * pair * P, 2 * (pair + 1) * P)
+        def divide(group):
+            queries = slice(group.start * P, group.stop * P)
             out_sb = work.tile([E, 2 * P], F32, name="out_sb")
-            nc.vector.tensor_tensor(out_sb[:], out_banks[pair][:], divisor[:, queries], MULT)
-            nc.sync.dma_start(out[:, queries], out_sb[:])
+            nc.vector.tensor_tensor(out_sb[:, : len(group) * P], out_banks[group][:], divisor[:, queries], MULT)
+            nc.sync.dma_start(out[:, queries], out_sb[:, : len(group) * P])
 
-        first_half, third_pair, last_pair = range(0, 4), range(4, 6), range(6, 8)
         for block in range(N_BLOCKS):
             exponentials(block)
             if block == 5:
-                invert_sums(first_half)
+                invert_sums(range(0, 4))
 
         vT = held.tile([P, N], BF16, name="vT")
         for piece in range(N_PIECES):
@@ -218,22 +219,23 @@ def tile_longformerselfattention_kernel(tc, table, wq, wk, wv, bq, bv, offs, out
                 nc.tensor.matmul(vT_ps[:, b * P : (b + 1) * P], v_sb[:, block * P : (block + 1) * P], ident[:], start=True, stop=True)
             nc.vector.tensor_copy(vT[:, piece * PIECE : (piece + 1) * PIECE], vT_ps[:])
 
-        invert_sums(third_pair)
-        flip(0)
-        flip(1)
-        first_half_ps = flip_sums(first_half)
-        copy_divisors(first_half, first_half_ps)
-        flip(2)
-        product(0)
-        third_pair_ps = flip_sums(third_pair)
-        copy_divisors(third_pair, third_pair_ps)
-        divide(0)
-        invert_sums(last_pair)
-        flip(3)
-        product(1)
-        last_pair_ps = flip_sums(last_pair)
-        copy_divisors(last_pair, last_pair_ps)
-        product(2)
-        product(3)
-        for pair in (1, 2, 3):
-            divide(pair)
+        groups = range(0, 2), range(2, 4), range(4, 6), range(6, 7), range(7, 8)
+        invert_sums(range(4, 6))
+        flip(groups[0])
+        flip(groups[1])
+        divisor_0_ps = flip_sums(range(0, 4))
+        copy_divisors(range(0, 4), divisor_0_ps)
+        flip(groups[2])
+        flip(groups[3])
+        product(groups[0])
+        divisor_1_ps = flip_sums(range(4, 6))
+        copy_divisors(range(4, 6), divisor_1_ps)
+        invert_sums(range(6, 8))
+        flip(groups[4])
+        product(groups[1])
+        divisor_2_ps = flip_sums(range(6, 8))
+        copy_divisors(range(6, 8), divisor_2_ps)
+        for group in groups[2:]:
+            product(group)
+        for group in groups:
+            divide(group)

import math

import concourse.mybir as mybir

BF16, F32, I32, U16 = mybir.dt.bfloat16, mybir.dt.float32, mybir.dt.int32, mybir.dt.uint16
ADD, MULT, IS_GT, IS_EQUAL = mybir.AluOpType.add, mybir.AluOpType.mult, mybir.AluOpType.is_gt, mybir.AluOpType.is_equal
EXP = mybir.ActivationFunctionType.Exp
IDENTITY = mybir.ActivationFunctionType.Identity
ALONG_FREE = mybir.AxisListType.X

P = 128
V, E, N = 512, 128, 1024
W = 128
PIECE = 512
N_PIECES = N // PIECE
N_BLOCKS = N // P
BLOCKS_PER_PIECE = PIECE // P
MASKED = -1.0e30

PAIRS_IN_BAND = N * (2 * W + 1) - W * (W + 1)
FLOPS = 3 * 2 * E * E * N + 2 * 2 * E * PAIRS_IN_BAND


def tile_longformerselfattention_kernel(tc, table, wq, wk, wv, bq, bv, offs, out):
    nc = tc.nc
    with (
        tc.tile_pool(name="lists", bufs=1) as lists,
        tc.tile_pool(name="held", bufs=1) as held,
        tc.tile_pool(name="held_per_block", bufs=N_BLOCKS) as held_per_block,
        tc.tile_pool(name="work", bufs=6) as work,
        tc.tile_pool(name="stats", bufs=8) as stats,
        tc.psum_pool(name="score_banks", bufs=4) as score_banks,
        tc.psum_pool(name="flipped", bufs=2) as flipped,
        tc.psum_pool(name="sums", bufs=2) as sums,
    ):
        table_rows = held.tile([P, V // P, E], BF16, name="table_rows")
        table_view = table.rearrange("(r p) d -> p r d", p=P)
        offsets = lists.tile([P, N // 16], U16, name="offsets")
        wq_sb = held.tile([E, E], BF16, name="wq_sb")
        wk_sb = held.tile([E, E], BF16, name="wk_sb")
        wv_sb = held.tile([E, E], BF16, name="wv_sb")
        bq_sb = held.tile([E, 1], F32, name="bq_sb")
        bv_sb = held.tile([E, 1], F32, name="bv_sb")
        nc.sync.dma_start(table_rows[:, 0:2, :], table_view[:, 0:2, :])
        nc.scalar.dma_start(table_rows[:, 2:4, :], table_view[:, 2:4, :])
        nc.sync.dma_start(offsets[:], offs)
        nc.scalar.dma_start(wk_sb[:], wk)
        with nc.allow_non_contiguous_dma(reason="one float32 of a bias to each partition"):
            nc.sync.dma_start(bq_sb[:], bq)
        nc.scalar.dma_start(wq_sb[:], wq)
        nc.sync.dma_start(wv_sb[:], wv)
        with nc.allow_non_contiguous_dma(reason="one float32 of a bias to each partition"):
            nc.scalar.dma_start(bv_sb[:], bv)

        warm = stats.tile([P, 1], F32, name="warm")
        nc.vector.memset(warm[:], 0.0)
        nc.scalar.activation(warm[:], warm[:], EXP)

        distance = held.tile([P, 2 * P], I32, name="distance")
        nc.gpsimd.iota(distance[:], pattern=[[2 * P, 2], [1, P]], base=-P, channel_multiplier=-1)
        distance_sq = held.tile([P, 2 * P], F32, name="distance_sq")
        nc.vector.tensor_tensor(distance_sq[:], distance[:], distance[:], MULT)
        band_mask = held.tile([P, 2 * P], BF16, name="band_mask")
        nc.vector.tensor_scalar(band_mask[:], distance_sq[:], float(W * W), MASKED, op0=IS_GT, op1=MULT)
        ident = held.tile([P, P], BF16, name="ident")
        nc.vector.tensor_scalar(ident[:], distance[:, :P], float(-P), None, op0=IS_EQUAL)
        ident_f32 = held.tile([P, P], F32, name="ident_f32")
        nc.vector.tensor_copy(ident_f32[:], ident[:])

        tableT_ps = flipped.tile([E, V], BF16, name="tableT_ps", tag="flipped")
        for r in range(V // P):
            nc.tensor.transpose(tableT_ps[:, r * P : (r + 1) * P], table_rows[:, r, :], ident[:])
        tableT = held.tile([E, V], BF16, name="tableT")
        nc.vector.tensor_copy(tableT[:], tableT_ps[:])

        q_sb = held.tile([E, N], BF16, name="q_sb")
        key_sb = held.tile([E, N], BF16, name="key_sb")
        v_sb = held.tile([E, N], BF16, name="v_sb")

        def project(weights, piece):
            looked_up = tableT[:].indirect(offsets[:, piece * (PIECE // 16) : (piece + 1) * (PIECE // 16)])
            borrowed, tag = ((flipped, "flipped"), (sums, "sums"))[piece]
            product = borrowed.tile([E, PIECE], F32, name="product", tag=tag)
            nc.tensor.matmul(product[:], weights[:], looked_up, start=True, stop=True)
            return product

        pieces = [slice(piece * PIECE, (piece + 1) * PIECE) for piece in range(N_PIECES)]
        for piece, cols in enumerate(pieces):
            nc.scalar.copy(key_sb[:, cols], project(wk_sb, piece)[:])
        for piece, cols in enumerate(pieces):
            nc.vector.tensor_scalar(
                q_sb[:, cols], project(wq_sb, piece)[:], bq_sb[:], 1.0 / math.sqrt(E), op0=ADD, op1=MULT
            )
        for piece, cols in enumerate(pieces):
            nc.scalar.activation(v_sb[:, cols], project(wv_sb, piece)[:], IDENTITY, bias=bv_sb[:], scale=1.0)

        key_by_block = key_sb[:].rearrange("c (k t) -> c k t", t=P)

        def neighbours_of(block):
            return [b for b in (block - 1, block + 1) if 0 <= b < N_BLOCKS]

        probs, probTs, out_banks = [], {}, {}
        exp_sums = held.tile([P, N_BLOCKS], F32, name="exp_sums")
        inv_sums = held.tile([P, N_BLOCKS], F32, name="inv_sums")
        divisor = held.tile([E, N], F32, name="divisor")
        def invert_sums(blocks):
            nc.vector.reciprocal(inv_sums[:, blocks.start : blocks.stop], exp_sums[:, blocks.start : blocks.stop])

        def flip_sums(blocks):
            divisor_ps = flipped.tile([E, PIECE], F32, name="divisor_ps", tag="flipped")
            for i, block in enumerate(blocks):
                nc.tensor.transpose(
                    divisor_ps[:, i * P : (i + 1) * P],
                    inv_sums[:, block : block + 1].to_broadcast([P, E]),
                    ident_f32[:],
                )
            return divisor_ps

        def copy_divisors(blocks, divisor_ps):
            nc.scalar.copy(divisor[:, blocks.start * P : blocks.stop * P], divisor_ps[:, : len(blocks) * P])

        def exponentials(block):
            neighbours = neighbours_of(block)
            masked = len(neighbours) * P
            width = masked + P
            step = 2 if len(neighbours) == 2 else 1
            mask_from = 0 if neighbours[0] < block else P
            q_block = q_sb[:, block * P : (block + 1) * P]

            scores = score_banks.tile([P, 3 * P], F32, name="scores")
            scores_by_block = scores[:].rearrange("j (k t) -> j k t", t=P)
            nc.tensor.matmul(
                scores[:, :masked], ident[:], band_mask[:, mask_from : mask_from + masked], start=True, stop=False
            )
            nc.tensor.matmul(
                scores_by_block[:, : len(neighbours), :],
                q_block,
                key_by_block[:, neighbours[0] : neighbours[-1] + 1 : step, :],
                start=False,
                stop=False,
            )
            nc.tensor.matmul(
                scores[:, masked:width], q_block, key_sb[:, block * P : (block + 1) * P], start=False, stop=True
            )

            neg_max = stats.tile([P, 1], F32, name="neg_max")
            nc.vector.reduce_max(neg_max[:], scores[:, :width], axis=ALONG_FREE, negate=True)
            prob = held_per_block.tile([P, 3 * P], BF16, name="prob")
            nc.scalar.activation(
                prob[:, :width],
                scores[:, :width],
                EXP,
                bias=neg_max[:],
                scale=1.0,
                accum_out=exp_sums[:, block : block + 1],
            )
            probs.append(prob)

        def keys_of(group):
            seen = {}
            for block in group:
                for key_block in neighbours_of(block) + [block]:
                    seen.setdefault(key_block, []).append(block)
            return sorted(seen.items(), key=lambda item: -len(item[1]))

        def flip(group):
            pool, tag = (sums, "sums") if group.stop <= BLOCKS_PER_PIECE else (score_banks, "scores")
            probT_ps = pool.tile([P, 6 * P], BF16, name="probT_ps", tag=tag)
            done = 0
            for key_block, blocks in keys_of(group):
                for block in blocks:
                    k = (neighbours_of(block) + [block]).index(key_block)
                    nc.tensor.matmul(
                        probT_ps[:, done : done + P],
                        probs[block][:, k * P : (k + 1) * P],
                        ident[:],
                        start=True,
                        stop=True,
                    )
                    done += P
            probT = held_per_block.tile([P, 6 * P], BF16, name="probT")
            nc.vector.tensor_copy(probT[:, :done], probT_ps[:, :done])
            probTs[group] = probT

        def product(group):
            pool, tag = (sums, "sums") if group.stop <= BLOCKS_PER_PIECE else (score_banks, "scores")
            out_ps = pool.tile([E, len(group) * P], F32, name="out_ps", tag=tag)
            done = 0
            terms = keys_of(group)
            for i, (key_block, blocks) in enumerate(terms):
                first_query = (blocks[0] - group.start) * P
                width = len(blocks) * P
                nc.tensor.matmul(
                    out_ps[:, first_query : first_query + width],
                    vT[:, key_block * P : (key_block + 1) * P],
                    probTs[group][:, done : done + width],
                    start=(i == 0),
                    stop=(i == len(terms) - 1),
                )
                done += width
            out_banks[group] = out_ps

        def divide(group):
            queries = slice(group.start * P, group.stop * P)
            out_sb = work.tile([E, 2 * P], F32, name="out_sb")
            nc.vector.tensor_tensor(out_sb[:, : len(group) * P], out_banks[group][:], divisor[:, queries], MULT)
            nc.sync.dma_start(out[:, queries], out_sb[:, : len(group) * P])

        for block in range(N_BLOCKS):
            exponentials(block)
            if block == 5:
                invert_sums(range(0, 4))

        vT = held.tile([P, N], BF16, name="vT")
        for piece in range(N_PIECES):
            vT_ps = flipped.tile([P, PIECE], BF16, name="vT_ps", tag="flipped")
            for b in range(BLOCKS_PER_PIECE):
                block = piece * BLOCKS_PER_PIECE + b
                nc.tensor.matmul(vT_ps[:, b * P : (b + 1) * P], v_sb[:, block * P : (block + 1) * P], ident[:], start=True, stop=True)
            nc.vector.tensor_copy(vT[:, piece * PIECE : (piece + 1) * PIECE], vT_ps[:])

        groups = range(0, 2), range(2, 4), range(4, 6), range(6, 7), range(7, 8)
        invert_sums(range(4, 6))
        flip(groups[0])
        flip(groups[1])
        divisor_0_ps = flip_sums(range(0, 4))
        copy_divisors(range(0, 4), divisor_0_ps)
        flip(groups[2])
        flip(groups[3])
        product(groups[0])
        divisor_1_ps = flip_sums(range(4, 6))
        copy_divisors(range(4, 6), divisor_1_ps)
        invert_sums(range(6, 8))
        flip(groups[4])
        product(groups[1])
        divisor_2_ps = flip_sums(range(6, 8))
        copy_divisors(range(6, 8), divisor_2_ps)
        for group in groups[2:]:
            product(group)
        for group in groups:
            divide(group)
